import numpy as np
import ml_dtypes


def mxq(x, axis, fmt="e4m3"):
    dtype, down = {"e4m3": (ml_dtypes.float8_e4m3fn, 7), "e5m2": (ml_dtypes.float8_e5m2, 14)}[fmt]
    v = np.moveaxis(np.asarray(x, np.float32).astype(ml_dtypes.bfloat16).astype(np.float64), axis, -1)
    blocks = v.reshape(v.shape[:-1] + (-1, 32))
    amax = np.abs(blocks).max(-1, keepdims=True)
    byte = np.maximum(np.where(amax > 0, np.frexp(amax)[1] - 1 + 127, 0) - down, 1)
    scale = np.exp2(byte - 127.0)
    codes = (blocks / scale).astype(np.float32).astype(dtype).astype(np.float64)
    return np.moveaxis((codes * scale).reshape(v.shape), -1, axis)


WIDE = False


def mx_kscale(k):
    if not WIDE:
        return np.ones(k)
    levels = np.array([10, -10, 5, -5, 0])
    a = np.random.permutation(np.resize(levels, k // 512 * 4)).reshape(k // 512, 4)
    idx = np.arange(k)
    return np.exp2(a[idx // 512, idx % 128 // 32])


BF16 = ml_dtypes.bfloat16


def bf(x):
    return np.asarray(x, np.float32).astype(BF16)


def f64(x):
    return np.asarray(x).astype(np.float64)


B, D, S, N = 4096, 1024, 2, 128
DS = D // S
EPS = 1e-12


def setup_inputs():
    s, t = mx_kscale(D), mx_kscale(D)
    return {"h": bf(np.random.standard_normal((B, D)) * s),
            "x2f": bf(np.random.standard_normal((B, D)) * t),
            "vu": bf(np.random.standard_normal((N, S, DS)) * 2.0 / np.sqrt(DS) / t.reshape(S, DS)),
            "w_f": bf(np.random.standard_normal((D, D)) / np.sqrt(D) * t[:, None] / s),
            "b_f": bf(np.random.standard_normal(D) * 0.2 * t),
            "bh": bf(1.0 + 0.1 * np.random.standard_normal(1)),
            "bx": bf(1.0 + 0.1 * np.random.standard_normal(1))}


def reference(h, x2f, vu, w_f, b_f, bh, bx):
    h2f = (mxq(f64(h), 1, "e4m3") @ mxq(f64(w_f), 1, "e4m3").T) + f64(b_f)
    vuq = mxq(f64(vu), 2, "e4m3").transpose(1, 2, 0)
    ah = (mxq(f64(x2f).reshape(B, S, DS), 2, "e4m3").transpose(1, 0, 2) @ vuq).transpose(1, 2, 0)
    ax = (mxq(h2f.reshape(B, S, DS), 2, "e4m3").transpose(1, 0, 2) @ vuq).transpose(1, 2, 0)
    ah = np.maximum(ah + f64(bh), 0.0)
    ax = np.maximum(ax + f64(bx), 0.0)
    a2 = (ah + ax) ** 2
    return a2 / np.maximum(a2.sum(axis=1, keepdims=True), EPS)

@@ -1,0 +1,322 @@
+from contextlib import ExitStack
+
+import concourse.mybir as mybir
+from concourse.masks import make_identity
+
+F32 = mybir.dt.float32
+BF16 = mybir.dt.bfloat16
+U32 = mybir.dt.uint32
+U8 = mybir.dt.uint8
+FP8X4 = mybir.dt.float8_e4m3fn_x4
+ALU = mybir.AluOpType
+ACT = mybir.ActivationFunctionType
+
+P = 128
+ROWS = 4096
+FEATURES = 1024
+ROLES = 128
+EPS = 1e-12
+
+PACK = 4
+HALVES = 2
+PAIR = 2
+SPAN = P * PACK
+SPANS = FEATURES // SPAN
+ROW_WORDS = FEATURES // PAIR
+
+ROUND_TILES = 2
+ROUNDS = ROWS // (P * ROUND_TILES)
+CHUNK_TILES = 4
+ROUNDS_PER_CHUNK = CHUNK_TILES // ROUND_TILES
+CHUNKS = ROWS // (P * CHUNK_TILES)
+CHUNK_BUFS = 4
+ROUND_COLS = ROUND_TILES * FEATURES
+SCORE_COLS = ROUND_TILES * SPANS * ROLES
+
+FLOPS = 2 * ROWS * FEATURES * FEATURES + 2 * 2 * ROWS * FEATURES * ROLES
+
+
+def tile_tpru_pa_t_kernel(tc, h, x2f, vu, w_f, b_f, bh, bx, out):
+    nc = tc.nc
+    with ExitStack() as ctx:
+        const = ctx.enter_context(tc.tile_pool(name="const", bufs=1))
+        rows_pool = ctx.enter_context(tc.tile_pool(name="rows", bufs=CHUNK_BUFS))
+        grouped_pool = ctx.enter_context(tc.tile_pool(name="grouped", bufs=2))
+        codes_pool = ctx.enter_context(tc.tile_pool(name="codes", bufs=3))
+        tail_pool = ctx.enter_context(tc.tile_pool(name="tail", bufs=2))
+        flip_psum = ctx.enter_context(tc.psum_pool(name="flip_psum", bufs=3))
+        h2f_psum = ctx.enter_context(tc.psum_pool(name="h2f_psum", bufs=3))
+        score_psum = ctx.enter_context(tc.psum_pool(name="score_psum", bufs=1))
+        ctx.enter_context(tc.manual_schedule())
+
+        h_chunks = h.rearrange("(c p j) k -> c p (j k)", p=P, j=CHUNK_TILES)
+        x_chunks = x2f.rearrange("(c p j) k -> c p (j k)", p=P, j=CHUNK_TILES)
+        out_chunks = out.rearrange("(c p j) n s -> c p (j n s)", p=P, j=CHUNK_TILES)
+
+        rows = {}
+        grouped = {}
+        codes = {}
+        scales = {}
+        scores = {}
+        tail = {}
+
+        def live(i):
+            return 0 <= i < ROUNDS
+
+        def load_chunk(c):
+            h_rows = rows_pool.tile([P, CHUNK_TILES * FEATURES], BF16)
+            nc.sync.dma_start(out=h_rows[:], in_=h_chunks[c])
+            x_rows = rows_pool.tile([P, CHUNK_TILES * FEATURES], BF16)
+            nc.sync.dma_start(out=x_rows[:], in_=x_chunks[c])
+            rows["h", c] = h_rows
+            rows["x", c] = x_rows
+
+        def word_tiles(values, tiles):
+            return values[:].bitcast(F32).rearrange(
+                "p (j g r u) -> p j g r u", j=tiles, g=SPANS, r=P, u=HALVES
+            )
+
+        def flip_tile(row_words, grouped_words, copy):
+            flipped = flip_psum.tile([P, SPANS, HALVES, P], F32)
+            for g in range(SPANS):
+                for u in range(HALVES):
+                    first = (g * HALVES + u) * P
+                    nc.tensor.transpose(
+                        flipped[:, g, u, :], row_words[:, first : first + P], identity[:]
+                    )
+            copy(out=grouped_words, in_=flipped[:].rearrange("p g u r -> p g r u"))
+
+        identity = const.tile([P, P], F32)
+        make_identity(nc, identity[:])
+
+        w_rows = const.tile([P, SPANS * PACK * FEATURES], BF16)
+        for s in range(SPANS):
+            nc.sync.dma_start(
+                out=w_rows[:, s * PACK * FEATURES : (s + 1) * PACK * FEATURES].rearrange(
+                    "c (u ek) -> c u ek", u=HALVES
+                ),
+                in_=w_f[s * SPAN : (s + 1) * SPAN, :].rearrange(
+                    "(u c e) k -> c u (e k)", u=HALVES, c=P, e=PAIR
+                ),
+            )
+        for c in range(CHUNK_BUFS):
+            load_chunk(c)
+
+        vu_rows = const.tile([P, FEATURES], BF16)
+        nc.scalar.dma_start(out=vu_rows[:], in_=vu.rearrange("n s d -> n (s d)"))
+        bias = const.tile([P, SPANS * PACK], BF16)
+        nc.scalar.dma_start(
+            out=bias[:].rearrange("c (m e) -> c m e", e=PAIR),
+            in_=b_f.rearrange("(m c e) -> c m e", m=SPANS * HALVES, c=P, e=PAIR),
+        )
+        bh_raw = const.tile([P, 1], BF16)
+        nc.scalar.dma_start(out=bh_raw[:], in_=bh.partition_broadcast(P))
+        bx_raw = const.tile([P, 1], BF16)
+        nc.scalar.dma_start(out=bx_raw[:], in_=bx.partition_broadcast(P))
+
+        w_words = w_rows[:].bitcast(F32)
+        w_grouped = const.tile([P, SPANS * PACK * FEATURES], BF16, align_bytes=64)
+        w_grouped_words = word_tiles(w_grouped, SPANS * PACK)
+        w_codes = const.tile([P, SPANS, PACK, SPANS, P], U32, align_bytes=64)
+        w_scales = const.tile([P, SPANS, PACK, SPANS, P], U8, align_bytes=64)
+        for s in range(SPANS):
+            for t in range(PACK):
+                m = s * PACK + t
+                flip_tile(
+                    w_words[:, m * ROW_WORDS : (m + 1) * ROW_WORDS],
+                    w_grouped_words[:, m],
+                    nc.scalar.copy if t % 2 == 0 else nc.vector.tensor_copy,
+                )
+            nc.vector.quantize_mx(
+                out=w_codes[:, s].rearrange("k t g c -> k (t g c)").bitcast(FP8X4),
+                scales=w_scales[:, s].rearrange("k t g c -> k (t g c)"),
+                in_=w_grouped[:, s * PACK * FEATURES : (s + 1) * PACK * FEATURES],
+            )
+
+        vu_grouped = const.tile([P, FEATURES], BF16, align_bytes=64)
+        vu_codes = const.tile([P, SPANS, ROLES], U32, align_bytes=64)
+        vu_scales = const.tile([P, SPANS, ROLES], U8, align_bytes=64)
+        flip_tile(vu_rows[:].bitcast(F32), word_tiles(vu_grouped, 1)[:, 0], nc.scalar.copy)
+        nc.vector.quantize_mx(
+            out=vu_codes[:].rearrange("d s n -> d (s n)").bitcast(FP8X4),
+            scales=vu_scales[:].rearrange("d s n -> d (s n)"),
+            in_=vu_grouped[:],
+        )
+
+        bh_f32 = const.tile([P, 1], F32)
+        nc.vector.tensor_copy(out=bh_f32[:], in_=bh_raw[:])
+        bx_f32 = const.tile([P, 1], F32)
+        nc.vector.tensor_copy(out=bx_f32[:], in_=bx_raw[:])
+        minus_bx = const.tile([P, 1], F32)
+        nc.vector.tensor_scalar_mul(out=minus_bx[:], in0=bx_raw[:], scalar1=-1.0)
+
+        def flip_round(i):
+            if not live(i):
+                return
+            c, part = divmod(i, ROUNDS_PER_CHUNK)
+            for operand in ("h", "x"):
+                values = grouped_pool.tile(
+                    [P, ROUND_COLS], BF16, name=operand + "_grouped", align_bytes=64
+                )
+                grouped[operand, i] = values
+                row_words = rows[operand, c][:].bitcast(F32)
+                for j in range(ROUND_TILES):
+                    first = (part * ROUND_TILES + j) * ROW_WORDS
+                    flip_tile(
+                        row_words[:, first : first + ROW_WORDS],
+                        word_tiles(values, ROUND_TILES)[:, j],
+                        nc.scalar.copy,
+                    )
+
+        def quantise(operand, i):
+            if not live(i):
+                return
+            words = codes_pool.tile(
+                [P, ROUND_TILES, SPANS, P], U32, name=operand + "_codes", align_bytes=64
+            )
+            plane = codes_pool.tile(
+                [P, ROUND_TILES, SPANS, P], U8, name=operand + "_scales", align_bytes=64
+            )
+            nc.vector.quantize_mx(
+                out=words[:].rearrange("k j g r -> k (j g r)").bitcast(FP8X4),
+                scales=plane[:].rearrange("k j g r -> k (j g r)"),
+                in_=grouped[operand, i][:],
+            )
+            codes[operand, i] = words
+            scales[operand, i] = plane
+
+        def project(i, j, s):
+            if not live(i):
+                return
+            if (j, s) == (0, 0):
+                h2f_grouped = grouped_pool.tile([P, ROUND_COLS], BF16, align_bytes=64)
+                grouped["h2f", i] = h2f_grouped
+            sums = h2f_psum.tile([P, PACK, P], F32)
+            for t in range(PACK):
+                for g in range(SPANS):
+                    nc.tensor.matmul_mx(
+                        out=sums[:, t, :],
+                        lhsT=w_codes[:, s, t, g, :].bitcast(FP8X4),
+                        lhsT_scale=w_scales[:, s, t, g, :],
+                        rhs=codes["h", i][:, j, g, :].bitcast(FP8X4),
+                        rhs_scale=scales["h", i][:, j, g, :],
+                        start=(g == 0),
+                        stop=(g == SPANS - 1),
+                    )
+            nc.vector.tensor_tensor(
+                out=grouped["h2f", i][:].rearrange(
+                    "c (j s r t) -> c j s r t", j=ROUND_TILES, s=SPANS, r=P, t=PACK
+                )[:, j, s],
+                in0=sums[:].rearrange("c t r -> c r t"),
+                in1=bias[:, s * PACK : (s + 1) * PACK].unsqueeze(1).to_broadcast([P, P, PACK]),
+                op=ALU.add,
+            )
+
+        def score(i):
+            if not live(i):
+                return
+            for operand in ("x", "h2f"):
+                bank = score_psum.tile(
+                    [P, ROUND_TILES, SPANS, ROLES], F32, name=operand + "_scores"
+                )
+                scores[operand, i] = bank
+                for j in range(ROUND_TILES):
+                    for s in range(SPANS):
+                        nc.tensor.matmul_mx(
+                            out=bank[:, j, s, :],
+                            lhsT=codes[operand, i][:, j, s, :].bitcast(FP8X4),
+                            lhsT_scale=scales[operand, i][:, j, s, :],
+                            rhs=vu_codes[:, s, :].bitcast(FP8X4),
+                            rhs_scale=vu_scales[:, s, :],
+                            start=True,
+                            stop=True,
+                        )
+
+        def relu_x(i):
+            if not live(i):
+                return
+            ah = tail_pool.tile([P, SCORE_COLS], F32)
+            tail["ah", i] = ah
+            nc.scalar.activation(
+                out=ah[:],
+                in_=scores["x", i][:].rearrange("r j s n -> r (j s n)"),
+                func=ACT.Relu,
+                bias=bh_f32[:, 0:1],
+                scale=1.0,
+            )
+
+        def add_h(i):
+            if not live(i):
+                return
+            both = tail_pool.tile([P, SCORE_COLS], F32)
+            tail["both", i] = both
+            nc.vector.scalar_tensor_tensor(
+                out=both[:],
+                in0=scores["h2f", i][:].rearrange("r j s n -> r (j s n)"),
+                scalar=minus_bx[:, 0:1],
+                in1=tail["ah", i][:],
+                op0=ALU.max,
+                op1=ALU.add,
+            )
+
+        def square(i):
+            if not live(i):
+                return
+            a2 = tail_pool.tile([P, SCORE_COLS], F32)
+            totals = tail_pool.tile([P, ROUND_TILES * SPANS], F32)
+            tail["a2", i] = a2
+            tail["totals", i] = totals
+            for q in range(ROUND_TILES * SPANS):
+                nc.scalar.activation(
+                    out=a2[:, q * ROLES : (q + 1) * ROLES],
+                    in_=tail["both", i][:, q * ROLES : (q + 1) * ROLES],
+                    func=ACT.Square,
+                    bias=bx_f32[:, 0:1],
+                    scale=1.0,
+                    accum_out=totals[:, q : q + 1],
+                )
+
+        def normalise(i):
+            if not live(i):
+                return
+            floored = tail_pool.tile([P, ROUND_TILES * SPANS], F32)
+            nc.vector.tensor_scalar_max(out=floored[:], in0=tail["totals", i][:], scalar1=EPS)
+            inverse = tail_pool.tile([P, ROUND_TILES * SPANS], F32)
+            nc.vector.reciprocal(out=inverse[:], in_=floored[:])
+            result = tail_pool.tile([P, SCORE_COLS], F32)
+            nc.vector.tensor_tensor(
+                out=result[:].rearrange(
+                    "r (j n s) -> r j n s", j=ROUND_TILES, n=ROLES, s=SPANS
+                ),
+                in0=tail["a2", i][:].rearrange(
+                    "r (j s n) -> r j n s", j=ROUND_TILES, s=SPANS, n=ROLES
+                ),
+                in1=inverse[:]
+                .rearrange("r (j s) -> r j s", s=SPANS)
+                .unsqueeze(2)
+                .to_broadcast([P, ROUND_TILES, ROLES, SPANS]),
+                op=ALU.mult,
+            )
+            c, part = divmod(i, ROUNDS_PER_CHUNK)
+            nc.sync.dma_start(
+                out=out_chunks[c][:, part * SCORE_COLS : (part + 1) * SCORE_COLS], in_=result[:]
+            )
+
+        for k in range(-2, ROUNDS + 2):
+            relu_x(k - 1)
+            flip_round(k + 2)
+            quantise("h2f", k)
+            add_h(k - 1)
+            normalise(k - 2)
+            square(k - 1)
+            project(k + 1, 0, 0)
+            quantise("h", k + 2)
+            project(k + 1, 0, 1)
+            quantise("x", k + 2)
+            project(k + 1, 1, 0)
+            project(k + 1, 1, 1)
+            score(k)
+            if live(k + 2) and (k + 2) % ROUNDS_PER_CHUNK == ROUNDS_PER_CHUNK - 1:
+                next_chunk = (k + 2) // ROUNDS_PER_CHUNK + CHUNK_BUFS
+                if next_chunk < CHUNKS:
+                    load_chunk(next_chunk)

@@ -26,10 +26,7 @@ ROW_WORDS = FEATURES // PAIR
 
 ROUND_TILES = 2
 ROUNDS = ROWS // (P * ROUND_TILES)
-CHUNK_TILES = 4
-ROUNDS_PER_CHUNK = CHUNK_TILES // ROUND_TILES
-CHUNKS = ROWS // (P * CHUNK_TILES)
-CHUNK_BUFS = 4
+ROW_BUFS = 6
 ROUND_COLS = ROUND_TILES * FEATURES
 SCORE_COLS = ROUND_TILES * SPANS * ROLES
 
@@ -40,18 +37,20 @@ def tile_tpru_pa_t_kernel(tc, h, x2f, vu, w_f, b_f, bh, bx, out):
     nc = tc.nc
     with ExitStack() as ctx:
         const = ctx.enter_context(tc.tile_pool(name="const", bufs=1))
-        rows_pool = ctx.enter_context(tc.tile_pool(name="rows", bufs=CHUNK_BUFS))
+        rows_pool = ctx.enter_context(tc.tile_pool(name="rows", bufs=ROW_BUFS))
         grouped_pool = ctx.enter_context(tc.tile_pool(name="grouped", bufs=2))
-        codes_pool = ctx.enter_context(tc.tile_pool(name="codes", bufs=3))
+        codes_pool = ctx.enter_context(tc.tile_pool(name="codes", bufs=2))
         tail_pool = ctx.enter_context(tc.tile_pool(name="tail", bufs=2))
         flip_psum = ctx.enter_context(tc.psum_pool(name="flip_psum", bufs=3))
         h2f_psum = ctx.enter_context(tc.psum_pool(name="h2f_psum", bufs=3))
         score_psum = ctx.enter_context(tc.psum_pool(name="score_psum", bufs=1))
         ctx.enter_context(tc.manual_schedule())
 
-        h_chunks = h.rearrange("(c p j) k -> c p (j k)", p=P, j=CHUNK_TILES)
-        x_chunks = x2f.rearrange("(c p j) k -> c p (j k)", p=P, j=CHUNK_TILES)
-        out_chunks = out.rearrange("(c p j) n s -> c p (j n s)", p=P, j=CHUNK_TILES)
+        dram_rounds = {
+            "h": h.rearrange("(i p j) k -> i p (j k)", p=P, j=ROUND_TILES),
+            "x": x2f.rearrange("(i p j) k -> i p (j k)", p=P, j=ROUND_TILES),
+            "out": out.rearrange("(i p j) n s -> i p (j n s)", p=P, j=ROUND_TILES),
+        }
 
         rows = {}
         grouped = {}
@@ -63,13 +62,12 @@ def tile_tpru_pa_t_kernel(tc, h, x2f, vu, w_f, b_f, bh, bx, out):
         def live(i):
             return 0 <= i < ROUNDS
 
-        def load_chunk(c):
-            h_rows = rows_pool.tile([P, CHUNK_TILES * FEATURES], BF16)
-            nc.sync.dma_start(out=h_rows[:], in_=h_chunks[c])
-            x_rows = rows_pool.tile([P, CHUNK_TILES * FEATURES], BF16)
-            nc.sync.dma_start(out=x_rows[:], in_=x_chunks[c])
-            rows["h", c] = h_rows
-            rows["x", c] = x_rows
+        def load(operand, i):
+            if not live(i):
+                return
+            loaded = rows_pool.tile([P, ROUND_COLS], BF16, name=operand + "_rows")
+            nc.sync.dma_start(out=loaded[:], in_=dram_rounds[operand][i])
+            rows[operand, i] = loaded
 
         def word_tiles(values, tiles):
             return values[:].bitcast(F32).rearrange(
@@ -99,8 +97,9 @@ def tile_tpru_pa_t_kernel(tc, h, x2f, vu, w_f, b_f, bh, bx, out):
                     "(u c e) k -> c u (e k)", u=HALVES, c=P, e=PAIR
                 ),
             )
-        for c in range(CHUNK_BUFS):
-            load_chunk(c)
+        for i in range(ROW_BUFS):
+            load("h", i)
+            load("x", i - 1)
 
         vu_rows = const.tile([P, FEATURES], BF16)
         nc.scalar.dma_start(out=vu_rows[:], in_=vu.rearrange("n s d -> n (s d)"))
@@ -150,23 +149,21 @@ def tile_tpru_pa_t_kernel(tc, h, x2f, vu, w_f, b_f, bh, bx, out):
         minus_bx = const.tile([P, 1], F32)
         nc.vector.tensor_scalar_mul(out=minus_bx[:], in0=bx_raw[:], scalar1=-1.0)
 
-        def flip_round(i):
+        def flip(operand, i):
             if not live(i):
                 return
-            c, part = divmod(i, ROUNDS_PER_CHUNK)
-            for operand in ("h", "x"):
-                values = grouped_pool.tile(
-                    [P, ROUND_COLS], BF16, name=operand + "_grouped", align_bytes=64
+            values = grouped_pool.tile(
+                [P, ROUND_COLS], BF16, name=operand + "_grouped", align_bytes=64
+            )
+            grouped[operand, i] = values
+            row_words = rows[operand, i][:].bitcast(F32)
+            for j in range(ROUND_TILES):
+                flip_tile(
+                    row_words[:, j * ROW_WORDS : (j + 1) * ROW_WORDS],
+                    word_tiles(values, ROUND_TILES)[:, j],
+                    nc.scalar.copy,
                 )
-                grouped[operand, i] = values
-                row_words = rows[operand, c][:].bitcast(F32)
-                for j in range(ROUND_TILES):
-                    first = (part * ROUND_TILES + j) * ROW_WORDS
-                    flip_tile(
-                        row_words[:, first : first + ROW_WORDS],
-                        word_tiles(values, ROUND_TILES)[:, j],
-                        nc.scalar.copy,
-                    )
+            load(operand, i + ROW_BUFS if operand == "h" else i + ROW_BUFS - 1)
 
         def quantise(operand, i):
             if not live(i):
@@ -276,13 +273,23 @@ def tile_tpru_pa_t_kernel(tc, h, x2f, vu, w_f, b_f, bh, bx, out):
                     accum_out=totals[:, q : q + 1],
                 )
 
-        def normalise(i):
+        def floor_totals(i):
             if not live(i):
                 return
             floored = tail_pool.tile([P, ROUND_TILES * SPANS], F32)
+            tail["floored", i] = floored
             nc.vector.tensor_scalar_max(out=floored[:], in0=tail["totals", i][:], scalar1=EPS)
+
+        def invert_totals(i):
+            if not live(i):
+                return
             inverse = tail_pool.tile([P, ROUND_TILES * SPANS], F32)
-            nc.vector.reciprocal(out=inverse[:], in_=floored[:])
+            tail["inverse", i] = inverse
+            nc.vector.reciprocal(out=inverse[:], in_=tail["floored", i][:])
+
+        def normalise(i):
+            if not live(i):
+                return
             result = tail_pool.tile([P, SCORE_COLS], F32)
             nc.vector.tensor_tensor(
                 out=result[:].rearrange(
@@ -291,32 +298,28 @@ def tile_tpru_pa_t_kernel(tc, h, x2f, vu, w_f, b_f, bh, bx, out):
                 in0=tail["a2", i][:].rearrange(
                     "r (j s n) -> r j n s", j=ROUND_TILES, s=SPANS, n=ROLES
                 ),
-                in1=inverse[:]
+                in1=tail["inverse", i][:]
                 .rearrange("r (j s) -> r j s", s=SPANS)
                 .unsqueeze(2)
                 .to_broadcast([P, ROUND_TILES, ROLES, SPANS]),
                 op=ALU.mult,
             )
-            c, part = divmod(i, ROUNDS_PER_CHUNK)
-            nc.sync.dma_start(
-                out=out_chunks[c][:, part * SCORE_COLS : (part + 1) * SCORE_COLS], in_=result[:]
-            )
+            nc.sync.dma_start(out=dram_rounds["out"][i], in_=result[:])
 
         for k in range(-2, ROUNDS + 2):
             relu_x(k - 1)
-            flip_round(k + 2)
-            quantise("h2f", k)
+            flip("h", k + 2)
+            flip("x", k + 1)
             add_h(k - 1)
-            normalise(k - 2)
+            floor_totals(k - 2)
+            quantise("h2f", k)
+            invert_totals(k - 2)
             square(k - 1)
             project(k + 1, 0, 0)
+            normalise(k - 2)
             quantise("h", k + 2)
             project(k + 1, 0, 1)
-            quantise("x", k + 2)
+            quantise("x", k + 1)
             project(k + 1, 1, 0)
             project(k + 1, 1, 1)
             score(k)
-            if live(k + 2) and (k + 2) % ROUNDS_PER_CHUNK == ROUNDS_PER_CHUNK - 1:
-                next_chunk = (k + 2) // ROUNDS_PER_CHUNK + CHUNK_BUFS
-                if next_chunk < CHUNKS:
-                    load_chunk(next_chunk)

@@ -291,7 +291,7 @@ def tile_tpru_pa_t_kernel(tc, h, x2f, vu, w_f, b_f, bh, bx, out):
             if not live(i):
                 return
             result = tail_pool.tile([P, SCORE_COLS], F32)
-            nc.vector.tensor_tensor(
+            nc.gpsimd.tensor_tensor(
                 out=result[:].rearrange(
                     "r (j n s) -> r j n s", j=ROUND_TILES, n=ROLES, s=SPANS
                 ),
@@ -306,20 +306,20 @@ def tile_tpru_pa_t_kernel(tc, h, x2f, vu, w_f, b_f, bh, bx, out):
             )
             nc.sync.dma_start(out=dram_rounds["out"][i], in_=result[:])
 
-        for k in range(-2, ROUNDS + 2):
-            relu_x(k - 1)
-            flip("h", k + 2)
-            flip("x", k + 1)
-            add_h(k - 1)
-            floor_totals(k - 2)
+        for k in range(-3, ROUNDS + 3):
+            quantise("h", k + 1)
             quantise("h2f", k)
-            invert_totals(k - 2)
-            square(k - 1)
+            quantise("x", k)
+            invert_totals(k - 3)
+            normalise(k - 3)
             project(k + 1, 0, 0)
-            normalise(k - 2)
-            quantise("h", k + 2)
+            add_h(k - 1)
             project(k + 1, 0, 1)
-            quantise("x", k + 1)
             project(k + 1, 1, 0)
             project(k + 1, 1, 1)
+            floor_totals(k - 2)
             score(k)
+            flip("h", k + 3)
+            relu_x(k)
+            flip("x", k + 2)
+            square(k - 1)

@@ -40,10 +40,9 @@ def tile_tpru_pa_t_kernel(tc, h, x2f, vu, w_f, b_f, bh, bx, out):
         rows_pool = ctx.enter_context(tc.tile_pool(name="rows", bufs=ROW_BUFS))
         grouped_pool = ctx.enter_context(tc.tile_pool(name="grouped", bufs=2))
         codes_pool = ctx.enter_context(tc.tile_pool(name="codes", bufs=2))
-        tail_pool = ctx.enter_context(tc.tile_pool(name="tail", bufs=2))
-        flip_psum = ctx.enter_context(tc.psum_pool(name="flip_psum", bufs=3))
+        tail_pool = ctx.enter_context(tc.tile_pool(name="tail", bufs=3))
         h2f_psum = ctx.enter_context(tc.psum_pool(name="h2f_psum", bufs=3))
-        score_psum = ctx.enter_context(tc.psum_pool(name="score_psum", bufs=1))
+        turn_psum = ctx.enter_context(tc.psum_pool(name="turn_psum", bufs=5))
         ctx.enter_context(tc.manual_schedule())
 
         dram_rounds = {
@@ -75,7 +74,7 @@ def tile_tpru_pa_t_kernel(tc, h, x2f, vu, w_f, b_f, bh, bx, out):
             )
 
         def flip_tile(row_words, grouped_words, copy):
-            flipped = flip_psum.tile([P, SPANS, HALVES, P], F32)
+            flipped = turn_psum.tile([P, SPANS, HALVES, P], F32, tag="turn")
             for g in range(SPANS):
                 for u in range(HALVES):
                     first = (g * HALVES + u) * P
@@ -86,20 +85,6 @@ def tile_tpru_pa_t_kernel(tc, h, x2f, vu, w_f, b_f, bh, bx, out):
 
         identity = const.tile([P, P], F32)
         make_identity(nc, identity[:])
-
-        w_rows = const.tile([P, SPANS * PACK * FEATURES], BF16)
-        for s in range(SPANS):
-            nc.sync.dma_start(
-                out=w_rows[:, s * PACK * FEATURES : (s + 1) * PACK * FEATURES].rearrange(
-                    "c (u ek) -> c u ek", u=HALVES
-                ),
-                in_=w_f[s * SPAN : (s + 1) * SPAN, :].rearrange(
-                    "(u c e) k -> c u (e k)", u=HALVES, c=P, e=PAIR
-                ),
-            )
-        for i in range(ROW_BUFS):
-            load("h", i)
-            load("x", i - 1)
 
         vu_rows = const.tile([P, FEATURES], BF16)
         nc.scalar.dma_start(out=vu_rows[:], in_=vu.rearrange("n s d -> n (s d)"))
@@ -112,6 +97,28 @@ def tile_tpru_pa_t_kernel(tc, h, x2f, vu, w_f, b_f, bh, bx, out):
         nc.scalar.dma_start(out=bh_raw[:], in_=bh.partition_broadcast(P))
         bx_raw = const.tile([P, 1], BF16)
         nc.scalar.dma_start(out=bx_raw[:], in_=bx.partition_broadcast(P))
+
+        w_rows = const.tile([P, SPANS * PACK * FEATURES], BF16)
+        for m in range(SPANS * HALVES):
+            nc.sync.dma_start(
+                out=w_rows[:, m * PAIR * FEATURES : (m + 1) * PAIR * FEATURES],
+                in_=w_f[m * P * PAIR : (m + 1) * P * PAIR, :].rearrange(
+                    "(c e) k -> c (e k)", c=P, e=PAIR
+                ),
+            )
+        for i in range(ROW_BUFS):
+            load("h", i)
+            load("x", i - 1)
+
+        vu_grouped = const.tile([P, FEATURES], BF16, align_bytes=64)
+        vu_codes = const.tile([P, SPANS, ROLES], U32, align_bytes=64)
+        vu_scales = const.tile([P, SPANS, ROLES], U8, align_bytes=64)
+        flip_tile(vu_rows[:].bitcast(F32), word_tiles(vu_grouped, 1)[:, 0], nc.scalar.copy)
+        nc.vector.quantize_mx(
+            out=vu_codes[:].rearrange("d s n -> d (s n)").bitcast(FP8X4),
+            scales=vu_scales[:].rearrange("d s n -> d (s n)"),
+            in_=vu_grouped[:],
+        )
 
         w_words = w_rows[:].bitcast(F32)
         w_grouped = const.tile([P, SPANS * PACK * FEATURES], BF16, align_bytes=64)
@@ -132,38 +139,26 @@ def tile_tpru_pa_t_kernel(tc, h, x2f, vu, w_f, b_f, bh, bx, out):
                 in_=w_grouped[:, s * PACK * FEATURES : (s + 1) * PACK * FEATURES],
             )
 
-        vu_grouped = const.tile([P, FEATURES], BF16, align_bytes=64)
-        vu_codes = const.tile([P, SPANS, ROLES], U32, align_bytes=64)
-        vu_scales = const.tile([P, SPANS, ROLES], U8, align_bytes=64)
-        flip_tile(vu_rows[:].bitcast(F32), word_tiles(vu_grouped, 1)[:, 0], nc.scalar.copy)
-        nc.vector.quantize_mx(
-            out=vu_codes[:].rearrange("d s n -> d (s n)").bitcast(FP8X4),
-            scales=vu_scales[:].rearrange("d s n -> d (s n)"),
-            in_=vu_grouped[:],
-        )
-
         bh_f32 = const.tile([P, 1], F32)
         nc.vector.tensor_copy(out=bh_f32[:], in_=bh_raw[:])
         bx_f32 = const.tile([P, 1], F32)
         nc.vector.tensor_copy(out=bx_f32[:], in_=bx_raw[:])
-        minus_bx = const.tile([P, 1], F32)
-        nc.vector.tensor_scalar_mul(out=minus_bx[:], in0=bx_raw[:], scalar1=-1.0)
+        score_bias = {"x": bh_f32, "h2f": bx_f32}
 
-        def flip(operand, i):
+        def flip(operand, i, j):
             if not live(i):
                 return
-            values = grouped_pool.tile(
-                [P, ROUND_COLS], BF16, name=operand + "_grouped", align_bytes=64
-            )
-            grouped[operand, i] = values
-            row_words = rows[operand, i][:].bitcast(F32)
-            for j in range(ROUND_TILES):
-                flip_tile(
-                    row_words[:, j * ROW_WORDS : (j + 1) * ROW_WORDS],
-                    word_tiles(values, ROUND_TILES)[:, j],
-                    nc.scalar.copy,
+            if j == 0:
+                grouped[operand, i] = grouped_pool.tile(
+                    [P, ROUND_COLS], BF16, name=operand + "_grouped", align_bytes=64
                 )
-            load(operand, i + ROW_BUFS if operand == "h" else i + ROW_BUFS - 1)
+            flip_tile(
+                rows[operand, i][:].bitcast(F32)[:, j * ROW_WORDS : (j + 1) * ROW_WORDS],
+                word_tiles(grouped[operand, i], ROUND_TILES)[:, j],
+                nc.scalar.copy,
+            )
+            if j == ROUND_TILES - 1:
+                load(operand, i + ROW_BUFS if operand == "h" else i + ROW_BUFS - 1)
 
         def quantise(operand, i):
             if not live(i):
@@ -213,8 +208,8 @@ def tile_tpru_pa_t_kernel(tc, h, x2f, vu, w_f, b_f, bh, bx, out):
             if not live(i):
                 return
             for operand in ("x", "h2f"):
-                bank = score_psum.tile(
-                    [P, ROUND_TILES, SPANS, ROLES], F32, name=operand + "_scores"
+                bank = turn_psum.tile(
+                    [P, ROUND_TILES, SPANS, ROLES], F32, name=operand + "_scores", tag="turn"
                 )
                 scores[operand, i] = bank
                 for j in range(ROUND_TILES):
@@ -229,31 +224,26 @@ def tile_tpru_pa_t_kernel(tc, h, x2f, vu, w_f, b_f, bh, bx, out):
                             stop=True,
                         )
 
-        def relu_x(i):
+        def relu(operand, i):
             if not live(i):
                 return
-            ah = tail_pool.tile([P, SCORE_COLS], F32)
-            tail["ah", i] = ah
+            kept = tail_pool.tile([P, SCORE_COLS], F32, name=operand + "_relu")
+            tail[operand, i] = kept
             nc.scalar.activation(
-                out=ah[:],
-                in_=scores["x", i][:].rearrange("r j s n -> r (j s n)"),
+                out=kept[:],
+                in_=scores[operand, i][:].rearrange("r j s n -> r (j s n)"),
                 func=ACT.Relu,
-                bias=bh_f32[:, 0:1],
+                bias=score_bias[operand][:, 0:1],
                 scale=1.0,
             )
 
-        def add_h(i):
+        def add(helper, i):
             if not live(i):
                 return
             both = tail_pool.tile([P, SCORE_COLS], F32)
             tail["both", i] = both
-            nc.vector.scalar_tensor_tensor(
-                out=both[:],
-                in0=scores["h2f", i][:].rearrange("r j s n -> r (j s n)"),
-                scalar=minus_bx[:, 0:1],
-                in1=tail["ah", i][:],
-                op0=ALU.max,
-                op1=ALU.add,
+            helper.tensor_tensor(
+                out=both[:], in0=tail["x", i][:], in1=tail["h2f", i][:], op=ALU.add
             )
 
         def square(i):
@@ -268,8 +258,6 @@ def tile_tpru_pa_t_kernel(tc, h, x2f, vu, w_f, b_f, bh, bx, out):
                     out=a2[:, q * ROLES : (q + 1) * ROLES],
                     in_=tail["both", i][:, q * ROLES : (q + 1) * ROLES],
                     func=ACT.Square,
-                    bias=bx_f32[:, 0:1],
-                    scale=1.0,
                     accum_out=totals[:, q : q + 1],
                 )
 
@@ -287,11 +275,11 @@ def tile_tpru_pa_t_kernel(tc, h, x2f, vu, w_f, b_f, bh, bx, out):
             tail["inverse", i] = inverse
             nc.vector.reciprocal(out=inverse[:], in_=tail["floored", i][:])
 
-        def normalise(i):
+        def normalise(helper, i):
             if not live(i):
                 return
             result = tail_pool.tile([P, SCORE_COLS], F32)
-            nc.gpsimd.tensor_tensor(
+            helper.tensor_tensor(
                 out=result[:].rearrange(
                     "r (j n s) -> r j n s", j=ROUND_TILES, n=ROLES, s=SPANS
                 ),
@@ -306,20 +294,23 @@ def tile_tpru_pa_t_kernel(tc, h, x2f, vu, w_f, b_f, bh, bx, out):
             )
             nc.sync.dma_start(out=dram_rounds["out"][i], in_=result[:])
 
-        for k in range(-3, ROUNDS + 3):
-            quantise("h", k + 1)
-            quantise("h2f", k)
-            quantise("x", k)
-            invert_totals(k - 3)
-            normalise(k - 3)
-            project(k + 1, 0, 0)
-            add_h(k - 1)
-            project(k + 1, 0, 1)
-            project(k + 1, 1, 0)
-            project(k + 1, 1, 1)
-            floor_totals(k - 2)
-            score(k)
-            flip("h", k + 3)
-            relu_x(k)
-            flip("x", k + 2)
+        for k in range(-3, ROUNDS + 2):
+            helper = nc.gpsimd if k < ROUNDS - 1 else nc.vector
+            add(helper, k - 1)
+            normalise(helper, k - 2)
             square(k - 1)
+            for j in range(ROUND_TILES):
+                for s in range(SPANS):
+                    project(k + 1, j, s)
+            floor_totals(k - 1)
+            quantise("h", k + 2)
+            quantise("x", k + 1)
+            quantise("h2f", k + 1)
+            invert_totals(k - 1)
+            score(k)
+            relu("x", k)
+            relu("h2f", k)
+            for j in range(ROUND_TILES):
+                flip("h", k + 3, j)
+            for j in range(ROUND_TILES):
+                flip("x", k + 2, j)

@@ -294,10 +294,9 @@ def tile_tpru_pa_t_kernel(tc, h, x2f, vu, w_f, b_f, bh, bx, out):
             )
             nc.sync.dma_start(out=dram_rounds["out"][i], in_=result[:])
 
-        for k in range(-3, ROUNDS + 2):
-            helper = nc.gpsimd if k < ROUNDS - 1 else nc.vector
-            add(helper, k - 1)
-            normalise(helper, k - 2)
+        for k in range(-3, ROUNDS - 1):
+            add(nc.gpsimd, k - 1)
+            normalise(nc.gpsimd, k - 2)
             square(k - 1)
             for j in range(ROUND_TILES):
                 for s in range(SPANS):
@@ -314,3 +313,19 @@ def tile_tpru_pa_t_kernel(tc, h, x2f, vu, w_f, b_f, bh, bx, out):
                 flip("h", k + 3, j)
             for j in range(ROUND_TILES):
                 flip("x", k + 2, j)
+
+        last = ROUNDS - 1
+        score(last)
+        relu("x", last)
+        relu("h2f", last)
+        add(nc.vector, last - 1)
+        normalise(nc.vector, last - 2)
+        square(last - 1)
+        add(nc.vector, last)
+        floor_totals(last - 1)
+        square(last)
+        invert_totals(last - 1)
+        normalise(nc.vector, last - 1)
+        floor_totals(last)
+        invert_totals(last)
+        normalise(nc.vector, last)

from contextlib import ExitStack

import concourse.mybir as mybir
from concourse.masks import make_identity

F32 = mybir.dt.float32
BF16 = mybir.dt.bfloat16
U32 = mybir.dt.uint32
U8 = mybir.dt.uint8
FP8X4 = mybir.dt.float8_e4m3fn_x4
ALU = mybir.AluOpType
ACT = mybir.ActivationFunctionType

P = 128
ROWS = 4096
FEATURES = 1024
ROLES = 128
EPS = 1e-12

PACK = 4
HALVES = 2
PAIR = 2
SPAN = P * PACK
SPANS = FEATURES // SPAN
ROW_WORDS = FEATURES // PAIR

ROUND_TILES = 2
ROUNDS = ROWS // (P * ROUND_TILES)
ROW_BUFS = 6
ROUND_COLS = ROUND_TILES * FEATURES
SCORE_COLS = ROUND_TILES * SPANS * ROLES

FLOPS = 2 * ROWS * FEATURES * FEATURES + 2 * 2 * ROWS * FEATURES * ROLES


def tile_tpru_pa_t_kernel(tc, h, x2f, vu, w_f, b_f, bh, bx, out):
    nc = tc.nc
    with ExitStack() as ctx:
        const = ctx.enter_context(tc.tile_pool(name="const", bufs=1))
        rows_pool = ctx.enter_context(tc.tile_pool(name="rows", bufs=ROW_BUFS))
        grouped_pool = ctx.enter_context(tc.tile_pool(name="grouped", bufs=2))
        codes_pool = ctx.enter_context(tc.tile_pool(name="codes", bufs=2))
        tail_pool = ctx.enter_context(tc.tile_pool(name="tail", bufs=3))
        h2f_psum = ctx.enter_context(tc.psum_pool(name="h2f_psum", bufs=3))
        turn_psum = ctx.enter_context(tc.psum_pool(name="turn_psum", bufs=5))
        ctx.enter_context(tc.manual_schedule())

        dram_rounds = {
            "h": h.rearrange("(i p j) k -> i p (j k)", p=P, j=ROUND_TILES),
            "x": x2f.rearrange("(i p j) k -> i p (j k)", p=P, j=ROUND_TILES),
            "out": out.rearrange("(i p j) n s -> i p (j n s)", p=P, j=ROUND_TILES),
        }

        rows = {}
        grouped = {}
        codes = {}
        scales = {}
        scores = {}
        tail = {}

        def live(i):
            return 0 <= i < ROUNDS

        def load(operand, i):
            if not live(i):
                return
            loaded = rows_pool.tile([P, ROUND_COLS], BF16, name=operand + "_rows")
            nc.sync.dma_start(out=loaded[:], in_=dram_rounds[operand][i])
            rows[operand, i] = loaded

        def word_tiles(values, tiles):
            return values[:].bitcast(F32).rearrange(
                "p (j g r u) -> p j g r u", j=tiles, g=SPANS, r=P, u=HALVES
            )

        def flip_tile(row_words, grouped_words, copy):
            flipped = turn_psum.tile([P, SPANS, HALVES, P], F32, tag="turn")
            for g in range(SPANS):
                for u in range(HALVES):
                    first = (g * HALVES + u) * P
                    nc.tensor.transpose(
                        flipped[:, g, u, :], row_words[:, first : first + P], identity[:]
                    )
            copy(out=grouped_words, in_=flipped[:].rearrange("p g u r -> p g r u"))

        identity = const.tile([P, P], F32)
        make_identity(nc, identity[:])

        vu_rows = const.tile([P, FEATURES], BF16)
        nc.scalar.dma_start(out=vu_rows[:], in_=vu.rearrange("n s d -> n (s d)"))
        bias = const.tile([P, SPANS * PACK], BF16)
        nc.scalar.dma_start(
            out=bias[:].rearrange("c (m e) -> c m e", e=PAIR),
            in_=b_f.rearrange("(m c e) -> c m e", m=SPANS * HALVES, c=P, e=PAIR),
        )
        bh_raw = const.tile([P, 1], BF16)
        nc.scalar.dma_start(out=bh_raw[:], in_=bh.partition_broadcast(P))
        bx_raw = const.tile([P, 1], BF16)
        nc.scalar.dma_start(out=bx_raw[:], in_=bx.partition_broadcast(P))

        w_rows = const.tile([P, SPANS * PACK * FEATURES], BF16)
        for m in range(SPANS * HALVES):
            nc.sync.dma_start(
                out=w_rows[:, m * PAIR * FEATURES : (m + 1) * PAIR * FEATURES],
                in_=w_f[m * P * PAIR : (m + 1) * P * PAIR, :].rearrange(
                    "(c e) k -> c (e k)", c=P, e=PAIR
                ),
            )
        for i in range(ROW_BUFS):
            load("h", i)
            load("x", i - 1)

        vu_grouped = const.tile([P, FEATURES], BF16, align_bytes=64)
        vu_codes = const.tile([P, SPANS, ROLES], U32, align_bytes=64)
        vu_scales = const.tile([P, SPANS, ROLES], U8, align_bytes=64)
        flip_tile(vu_rows[:].bitcast(F32), word_tiles(vu_grouped, 1)[:, 0], nc.scalar.copy)
        nc.vector.quantize_mx(
            out=vu_codes[:].rearrange("d s n -> d (s n)").bitcast(FP8X4),
            scales=vu_scales[:].rearrange("d s n -> d (s n)"),
            in_=vu_grouped[:],
        )

        w_words = w_rows[:].bitcast(F32)
        w_grouped = const.tile([P, SPANS * PACK * FEATURES], BF16, align_bytes=64)
        w_grouped_words = word_tiles(w_grouped, SPANS * PACK)
        w_codes = const.tile([P, SPANS, PACK, SPANS, P], U32, align_bytes=64)
        w_scales = const.tile([P, SPANS, PACK, SPANS, P], U8, align_bytes=64)
        for s in range(SPANS):
            for t in range(PACK):
                m = s * PACK + t
                flip_tile(
                    w_words[:, m * ROW_WORDS : (m + 1) * ROW_WORDS],
                    w_grouped_words[:, m],
                    nc.scalar.copy if t % 2 == 0 else nc.vector.tensor_copy,
                )
            nc.vector.quantize_mx(
                out=w_codes[:, s].rearrange("k t g c -> k (t g c)").bitcast(FP8X4),
                scales=w_scales[:, s].rearrange("k t g c -> k (t g c)"),
                in_=w_grouped[:, s * PACK * FEATURES : (s + 1) * PACK * FEATURES],
            )

        bh_f32 = const.tile([P, 1], F32)
        nc.vector.tensor_copy(out=bh_f32[:], in_=bh_raw[:])
        bx_f32 = const.tile([P, 1], F32)
        nc.vector.tensor_copy(out=bx_f32[:], in_=bx_raw[:])
        score_bias = {"x": bh_f32, "h2f": bx_f32}

        def flip(operand, i, j):
            if not live(i):
                return
            if j == 0:
                grouped[operand, i] = grouped_pool.tile(
                    [P, ROUND_COLS], BF16, name=operand + "_grouped", align_bytes=64
                )
            flip_tile(
                rows[operand, i][:].bitcast(F32)[:, j * ROW_WORDS : (j + 1) * ROW_WORDS],
                word_tiles(grouped[operand, i], ROUND_TILES)[:, j],
                nc.scalar.copy,
            )
            if j == ROUND_TILES - 1:
                load(operand, i + ROW_BUFS if operand == "h" else i + ROW_BUFS - 1)

        def quantise(operand, i):
            if not live(i):
                return
            words = codes_pool.tile(
                [P, ROUND_TILES, SPANS, P], U32, name=operand + "_codes", align_bytes=64
            )
            plane = codes_pool.tile(
                [P, ROUND_TILES, SPANS, P], U8, name=operand + "_scales", align_bytes=64
            )
            nc.vector.quantize_mx(
                out=words[:].rearrange("k j g r -> k (j g r)").bitcast(FP8X4),
                scales=plane[:].rearrange("k j g r -> k (j g r)"),
                in_=grouped[operand, i][:],
            )
            codes[operand, i] = words
            scales[operand, i] = plane

        def project(i, j, s):
            if not live(i):
                return
            if (j, s) == (0, 0):
                h2f_grouped = grouped_pool.tile([P, ROUND_COLS], BF16, align_bytes=64)
                grouped["h2f", i] = h2f_grouped
            sums = h2f_psum.tile([P, PACK, P], F32)
            for t in range(PACK):
                for g in range(SPANS):
                    nc.tensor.matmul_mx(
                        out=sums[:, t, :],
                        lhsT=w_codes[:, s, t, g, :].bitcast(FP8X4),
                        lhsT_scale=w_scales[:, s, t, g, :],
                        rhs=codes["h", i][:, j, g, :].bitcast(FP8X4),
                        rhs_scale=scales["h", i][:, j, g, :],
                        start=(g == 0),
                        stop=(g == SPANS - 1),
                    )
            nc.vector.tensor_tensor(
                out=grouped["h2f", i][:].rearrange(
                    "c (j s r t) -> c j s r t", j=ROUND_TILES, s=SPANS, r=P, t=PACK
                )[:, j, s],
                in0=sums[:].rearrange("c t r -> c r t"),
                in1=bias[:, s * PACK : (s + 1) * PACK].unsqueeze(1).to_broadcast([P, P, PACK]),
                op=ALU.add,
            )

        def score(i):
            if not live(i):
                return
            for operand in ("x", "h2f"):
                bank = turn_psum.tile(
                    [P, ROUND_TILES, SPANS, ROLES], F32, name=operand + "_scores", tag="turn"
                )
                scores[operand, i] = bank
                for j in range(ROUND_TILES):
                    for s in range(SPANS):
                        nc.tensor.matmul_mx(
                            out=bank[:, j, s, :],
                            lhsT=codes[operand, i][:, j, s, :].bitcast(FP8X4),
                            lhsT_scale=scales[operand, i][:, j, s, :],
                            rhs=vu_codes[:, s, :].bitcast(FP8X4),
                            rhs_scale=vu_scales[:, s, :],
                            start=True,
                            stop=True,
                        )

        def relu(operand, i):
            if not live(i):
                return
            kept = tail_pool.tile([P, SCORE_COLS], F32, name=operand + "_relu")
            tail[operand, i] = kept
            nc.scalar.activation(
                out=kept[:],
                in_=scores[operand, i][:].rearrange("r j s n -> r (j s n)"),
                func=ACT.Relu,
                bias=score_bias[operand][:, 0:1],
                scale=1.0,
            )

        def add(helper, i):
            if not live(i):
                return
            both = tail_pool.tile([P, SCORE_COLS], F32)
            tail["both", i] = both
            helper.tensor_tensor(
                out=both[:], in0=tail["x", i][:], in1=tail["h2f", i][:], op=ALU.add
            )

        def square(i):
            if not live(i):
                return
            a2 = tail_pool.tile([P, SCORE_COLS], F32)
            totals = tail_pool.tile([P, ROUND_TILES * SPANS], F32)
            tail["a2", i] = a2
            tail["totals", i] = totals
            for q in range(ROUND_TILES * SPANS):
                nc.scalar.activation(
                    out=a2[:, q * ROLES : (q + 1) * ROLES],
                    in_=tail["both", i][:, q * ROLES : (q + 1) * ROLES],
                    func=ACT.Square,
                    accum_out=totals[:, q : q + 1],
                )

        def floor_totals(i):
            if not live(i):
                return
            floored = tail_pool.tile([P, ROUND_TILES * SPANS], F32)
            tail["floored", i] = floored
            nc.vector.tensor_scalar_max(out=floored[:], in0=tail["totals", i][:], scalar1=EPS)

        def invert_totals(i):
            if not live(i):
                return
            inverse = tail_pool.tile([P, ROUND_TILES * SPANS], F32)
            tail["inverse", i] = inverse
            nc.vector.reciprocal(out=inverse[:], in_=tail["floored", i][:])

        def normalise(helper, i):
            if not live(i):
                return
            result = tail_pool.tile([P, SCORE_COLS], F32)
            helper.tensor_tensor(
                out=result[:].rearrange(
                    "r (j n s) -> r j n s", j=ROUND_TILES, n=ROLES, s=SPANS
                ),
                in0=tail["a2", i][:].rearrange(
                    "r (j s n) -> r j n s", j=ROUND_TILES, s=SPANS, n=ROLES
                ),
                in1=tail["inverse", i][:]
                .rearrange("r (j s) -> r j s", s=SPANS)
                .unsqueeze(2)
                .to_broadcast([P, ROUND_TILES, ROLES, SPANS]),
                op=ALU.mult,
            )
            nc.sync.dma_start(out=dram_rounds["out"][i], in_=result[:])

        for k in range(-3, ROUNDS - 1):
            add(nc.gpsimd, k - 1)
            normalise(nc.gpsimd, k - 2)
            square(k - 1)
            for j in range(ROUND_TILES):
                for s in range(SPANS):
                    project(k + 1, j, s)
            floor_totals(k - 1)
            quantise("h", k + 2)
            quantise("x", k + 1)
            quantise("h2f", k + 1)
            invert_totals(k - 1)
            score(k)
            relu("x", k)
            relu("h2f", k)
            for j in range(ROUND_TILES):
                flip("h", k + 3, j)
            for j in range(ROUND_TILES):
                flip("x", k + 2, j)

        last = ROUNDS - 1
        score(last)
        relu("x", last)
        relu("h2f", last)
        add(nc.vector, last - 1)
        normalise(nc.vector, last - 2)
        square(last - 1)
        add(nc.vector, last)
        floor_totals(last - 1)
        square(last)
        invert_totals(last - 1)
        normalise(nc.vector, last - 1)
        floor_totals(last)
        invert_totals(last)
        normalise(nc.vector, last)
